import numpy as np
import ml_dtypes


def mxq(x, axis, fmt="e4m3"):
    dtype, down = {"e4m3": (ml_dtypes.float8_e4m3fn, 7), "e5m2": (ml_dtypes.float8_e5m2, 14)}[fmt]
    v = np.moveaxis(np.asarray(x, np.float32).astype(ml_dtypes.bfloat16).astype(np.float64), axis, -1)
    blocks = v.reshape(v.shape[:-1] + (-1, 32))
    amax = np.abs(blocks).max(-1, keepdims=True)
    byte = np.maximum(np.where(amax > 0, np.frexp(amax)[1] - 1 + 127, 0) - down, 1)
    scale = np.exp2(byte - 127.0)
    codes = (blocks / scale).astype(np.float32).astype(dtype).astype(np.float64)
    return np.moveaxis((codes * scale).reshape(v.shape), -1, axis)


WIDE = False


def mx_kscale(k):
    if not WIDE:
        return np.ones(k)
    levels = np.array([10, -10, 5, -5, 0])
    a = np.random.permutation(np.resize(levels, k // 512 * 4)).reshape(k // 512, 4)
    idx = np.arange(k)
    return np.exp2(a[idx // 512, idx % 128 // 32])


BF16 = ml_dtypes.bfloat16


def bf(x):
    return np.asarray(x, np.float32).astype(BF16)


def f64(x):
    return np.asarray(x).astype(np.float64)


E2M1 = np.array([0.0, 0.5, 1.0, 1.5, 2.0, 3.0, 4.0, 6.0, -0.0, -0.5, -1.0, -1.5, -2.0, -3.0, -4.0, -6.0])


def pack_weight(w, fmt):
    k, n = w.shape
    w = f64(bf(w)).reshape(k // 32, 32, n)
    amax = np.abs(w).max(1)
    if fmt == "e4m3":
        byte = np.frexp(amax)[1] - 1 + 127 - 7
    else:
        mant, ex = np.frexp(amax / 6.0)
        byte = np.where(mant > 0.5, ex, ex - 1) + 127
    byte = np.clip(np.where(amax > 0, byte, 1), 1, 254)
    scaled = (w * np.exp2(127.0 - byte)[:, None, :]).reshape(k, n).astype(np.float32)
    by_word = np.ascontiguousarray(scaled.reshape(k // 512, 128, 4, n).transpose(0, 1, 3, 2))
    if fmt == "e4m3":
        words = by_word.astype(ml_dtypes.float8_e4m3fn).view(np.uint8)
    else:
        c = by_word.astype(ml_dtypes.float4_e2m1fn).view(np.uint8) & 0xF
        words = c[..., 0::2] | (c[..., 1::2] << 4)
    return np.ascontiguousarray(words), np.ascontiguousarray(byte.astype(np.uint8).reshape(k // 512, 16, n))


def unpack_weight(words, scales, fmt):
    g, p, n, _ = words.shape
    if fmt == "e4m3":
        vals = np.ascontiguousarray(words).view(ml_dtypes.float8_e4m3fn).astype(np.float64)
    else:
        nib = np.empty((g, p, n, 4), np.uint8)
        nib[..., 0::2] = words & 0xF
        nib[..., 1::2] = words >> 4
        vals = E2M1[nib]
    vals = vals * np.repeat(np.exp2(scales.astype(np.float64) - 127.0), 8, axis=1)[..., None]
    return vals.transpose(0, 1, 3, 2).reshape(g * 512, n)


def pack4(w):
    words, scales = pack_weight(w, "e2m1")
    return words.reshape(words.shape[0], 128, -1), scales


def unpack4(words, scales):
    return unpack_weight(words.reshape(words.shape[0], 128, -1, 2), scales, "e2m1")


B, S, H, F = 4, 32, 2048, 4096


def setup_inputs():
    s, t = mx_kscale(H), mx_kscale(F)
    x = bf(np.random.standard_normal((B, S, H)) * s)
    Wg = np.random.standard_normal((H, F)) * 0.022 / s[:, None]
    Wu = np.random.standard_normal((H, F)) * 0.022 / s[:, None] * t
    Wd = np.random.standard_normal((F, H)) * 0.025 / t[:, None]
    gate_W_words, gate_W_scales = pack4(Wg)
    up_W_words, up_W_scales = pack4(Wu)
    down_W_words, down_W_scales = pack4(Wd)
    return {"x": x,
            "gate_W_words": gate_W_words, "gate_W_scales": gate_W_scales,
            "up_W_words": up_W_words, "up_W_scales": up_W_scales,
            "down_W_words": down_W_words, "down_W_scales": down_W_scales}


def reference(x, gate_W_words, gate_W_scales, up_W_words, up_W_scales, down_W_words, down_W_scales):
    b, s_len, h = x.shape
    xt = f64(x).reshape(b * s_len, h)
    Wg = unpack4(gate_W_words, gate_W_scales)
    Wu = unpack4(up_W_words, up_W_scales)
    Wd = unpack4(down_W_words, down_W_scales)
    xq = mxq(xt, 1, "e4m3")
    gate = xq @ Wg
    up = xq @ Wu
    gelu = np.tanh(0.7978845608028654 * (gate + 0.044715 * gate ** 3)) * gate * 0.5 + gate * 0.5
    inter = gelu * up
    out = mxq(inter, 1, "e4m3") @ Wd
    return out.reshape(b, s_len, h)

@@ -1,0 +1,218 @@
+from contextlib import ExitStack
+
+import concourse.mybir as mybir
+from concourse.masks import make_identity
+
+F32 = mybir.dt.float32
+BF16 = mybir.dt.bfloat16
+I32 = mybir.dt.int32
+U32 = mybir.dt.uint32
+U8 = mybir.dt.uint8
+FP8X4 = mybir.dt.float8_e4m3fn_x4
+FP4X4 = mybir.dt.float4_e2m1fn_x4
+ACT = mybir.ActivationFunctionType
+ALU = mybir.AluOpType
+
+P = 128
+H = 2048
+F = 4096
+K_PASS = 512
+GH = H // K_PASS
+GF = F // K_PASS
+N_TILE = 512
+FT = F // N_TILE
+HT = H // N_TILE
+
+FLOPS = 2 * P * (2 * H * F + F * H)
+
+
+def load_scale_rows(nc, plane, scales, groups):
+    rows = scales.rearrange("g (h q) w -> q h g w", h=2)
+    for q in range(8):
+        first = 32 * (q // 4) + q % 4
+        nc.sync.dma_start(out=plane[first:P:64, groups, :], in_=rows[q, :, groups, :])
+
+
+def tile_w4a16tvmmlp_kernel(
+    tc,
+    x,
+    gate_W_words,
+    gate_W_scales,
+    up_W_words,
+    up_W_scales,
+    down_W_words,
+    down_W_scales,
+    out,
+):
+    nc = tc.nc
+    with ExitStack() as ctx:
+        keep = ctx.enter_context(tc.tile_pool(name="keep", bufs=1))
+        psum = ctx.enter_context(tc.psum_pool(name="psum", bufs=1))
+        ctx.enter_context(tc.manual_schedule())
+
+        def bank(i, dtype, name):
+            return psum.tile([P, N_TILE], dtype, tag="bank%d" % i, name=name)
+
+        x_sb = keep.tile([P, H], BF16, name="x_sb")
+        ident_f = keep.tile([P, P], F32, name="ident_f")
+        ident_b = keep.tile([P, P], BF16, name="ident_b")
+        warm = keep.tile([P, 8], F32, name="warm")
+        wg = keep.tile([P, GH * 2 * F], U8, name="wg", align_bytes=64)
+        wu = keep.tile([P, GH * 2 * F], U8, name="wu", align_bytes=64)
+        wd = keep.tile([P, GF * 2 * H], U8, name="wd", align_bytes=64)
+        sg = keep.tile([P, GH * F], U8, name="sg", align_bytes=64)
+        su = keep.tile([P, GH * F], U8, name="su", align_bytes=64)
+        sd = keep.tile([P, GF * H], U8, name="sd", align_bytes=64)
+        xg = keep.tile([P, GH * P * 4], BF16, name="xg", align_bytes=64)
+        xq = keep.tile([P, GH * P], U32, name="xq", align_bytes=64)
+        xs = keep.tile([P, GH * P], U8, name="xs", align_bytes=64)
+        gel = keep.tile([P, F], F32, name="gel")
+        inter = keep.tile([P, F], BF16, name="inter")
+        ig = keep.tile([P, GF * P * 4], BF16, name="ig", align_bytes=64)
+        iq = keep.tile([P, GF * P], U32, name="iq", align_bytes=64)
+        isc = keep.tile([P, GF * P], U8, name="isc", align_bytes=64)
+        osb = keep.tile([P, H], F32, name="osb")
+
+        wg_i = wg[:].bitcast(I32).rearrange("p (g w) -> p g w", g=GH)
+        wu_i = wu[:].bitcast(I32).rearrange("p (g w) -> p g w", g=GH)
+        wd_i = wd[:].bitcast(I32).rearrange("p (g w) -> p g w", g=GF)
+        sg_i = sg[:].bitcast(I32).rearrange("p (g w) -> p g w", g=GH)
+        su_i = su[:].bitcast(I32).rearrange("p (g w) -> p g w", g=GH)
+        sd_i = sd[:].bitcast(I32).rearrange("p (g w) -> p g w", g=GF)
+        gw_d = gate_W_words.bitcast(I32)
+        uw_d = up_W_words.bitcast(I32)
+        dw_d = down_W_words.bitcast(I32)
+        gs_d = gate_W_scales.bitcast(I32)
+        us_d = up_W_scales.bitcast(I32)
+        ds_d = down_W_scales.bitcast(I32)
+        out_flat = out.flatten_outer_dims()
+
+        nc.vector.memset(warm[:], 0.0)
+        nc.scalar.activation(out=warm[:], in_=warm[:], func=ACT.Gelu_apprx_tanh)
+        nc.vector.memset(sg[:].bitcast(I32), 0)
+        make_identity(nc, ident_f[:])
+        make_identity(nc, ident_b[:])
+
+        nc.sync.dma_start(out=x_sb[:], in_=x.flatten_outer_dims())
+        nc.sync.dma_start(out=wg_i[:, 0, :], in_=gw_d[0])
+        load_scale_rows(nc, sg_i, gs_d, slice(0, 2))
+        load_scale_rows(nc, sg_i, gs_d, slice(2, 4))
+        for g in range(1, GH):
+            nc.sync.dma_start(out=wg_i[:, g, :], in_=gw_d[g])
+
+        x_words = x_sb[:].bitcast(F32)
+        xg_words = xg[:].bitcast(F32)
+        for i in range(2):
+            xT = bank(i, F32, "xT%d" % i)
+            for gg in range(2):
+                g = 2 * i + gg
+                for u in range(2):
+                    col = P * (2 * gg + u)
+                    nc.tensor.transpose(
+                        xT[:, col : col + P],
+                        x_words[:, 256 * g + u : 256 * (g + 1) : 2],
+                        ident_f[:],
+                    )
+            dst = xg_words[:, 512 * i : 512 * (i + 1)].rearrange("p (g r u) -> p g r u", g=2, u=2)
+            src = xT[:].rearrange("p (g u r) -> p g r u", g=2, u=2)
+            if i == 0:
+                nc.vector.tensor_copy(out=dst, in_=src)
+            else:
+                nc.scalar.copy(out=dst, in_=src)
+        nc.vector.quantize_mx(out=xq[:].bitcast(FP8X4), scales=xs[:], in_=xg[:])
+
+        nc.vector.memset(su[:].bitcast(I32), 0)
+        load_scale_rows(nc, su_i, us_d, slice(0, 2))
+        load_scale_rows(nc, su_i, us_d, slice(2, 4))
+        half = F // 4
+        for h in range(2):
+            for g in range(GH):
+                nc.sync.dma_start(
+                    out=wu_i[:, g, half * h : half * (h + 1)],
+                    in_=uw_d[g][:, half * h : half * (h + 1)],
+                )
+        nc.vector.memset(sd[:].bitcast(I32), 0)
+        load_scale_rows(nc, sd_i, ds_d, slice(0, 4))
+        load_scale_rows(nc, sd_i, ds_d, slice(4, 8))
+        for g in range(GF - 1):
+            nc.sync.dma_start(out=wd_i[:, g, :], in_=dw_d[g])
+        piece = N_TILE // 2
+        for c in range(HT):
+            nc.sync.dma_start(
+                out=wd_i[:, GF - 1, piece * c : piece * (c + 1)],
+                in_=dw_d[GF - 1][:, piece * c : piece * (c + 1)],
+            )
+
+        def stage1_pass(acc, words, plane, g, j):
+            nc.tensor.matmul_mx(
+                out=acc[:],
+                lhsT=xq[:, P * g : P * (g + 1)].bitcast(FP8X4),
+                lhsT_scale=xs[:, P * g : P * (g + 1)],
+                rhs=words[:, 2 * F * g + 2 * N_TILE * j : 2 * F * g + 2 * N_TILE * (j + 1)].bitcast(FP4X4),
+                rhs_scale=plane[:, F * g + N_TILE * j : F * g + N_TILE * (j + 1)],
+                start=(g == 0),
+                stop=(g == GH - 1),
+            )
+
+        gate_acc = [bank(j, F32, "gate%d" % j) for j in range(FT)]
+        for g in range(GH):
+            for j in range(FT):
+                stage1_pass(gate_acc[j], wg, sg, g, j)
+        for j in range(FT):
+            nc.scalar.activation(
+                out=gel[:, N_TILE * j : N_TILE * (j + 1)],
+                in_=gate_acc[j][:],
+                func=ACT.Gelu_apprx_tanh,
+            )
+
+        up_acc = [bank(j, F32, "up%d" % j) for j in range(FT)]
+        for h in range(2):
+            tiles = range(4 * h, 4 * (h + 1))
+            for g in range(GH):
+                for j in tiles:
+                    stage1_pass(up_acc[j], wu, su, g, j)
+            for j in tiles:
+                nc.vector.tensor_tensor(
+                    out=inter[:, N_TILE * j : N_TILE * (j + 1)],
+                    in0=gel[:, N_TILE * j : N_TILE * (j + 1)],
+                    in1=up_acc[j][:],
+                    op=ALU.mult,
+                )
+
+        for j in range(GF):
+            iT = bank(j % 4, BF16, "iT%d" % j)
+            for t in range(4):
+                nc.tensor.transpose(
+                    iT[:, P * t : P * (t + 1)],
+                    inter[:, K_PASS * j + t : K_PASS * (j + 1) : 4],
+                    ident_b[:],
+                )
+            nc.scalar.copy(
+                out=ig[:, K_PASS * j : K_PASS * (j + 1)].rearrange("p (r t) -> p r t", t=4),
+                in_=iT[:].rearrange("p (t r) -> p r t", t=4),
+            )
+            nc.vector.quantize_mx(
+                out=iq[:, P * j : P * (j + 1)].bitcast(FP8X4),
+                scales=isc[:, P * j : P * (j + 1)],
+                in_=ig[:, K_PASS * j : K_PASS * (j + 1)],
+            )
+
+        out_acc = [bank(4 + c, F32, "out%d" % c) for c in range(HT)]
+        for g in range(GF):
+            for c in range(HT):
+                nc.tensor.matmul_mx(
+                    out=out_acc[c][:],
+                    lhsT=iq[:, P * g : P * (g + 1)].bitcast(FP8X4),
+                    lhsT_scale=isc[:, P * g : P * (g + 1)],
+                    rhs=wd[:, 2 * H * g + 2 * N_TILE * c : 2 * H * g + 2 * N_TILE * (c + 1)].bitcast(FP4X4),
+                    rhs_scale=sd[:, H * g + N_TILE * c : H * g + N_TILE * (c + 1)],
+                    start=(g == 0),
+                    stop=(g == GF - 1),
+                )
+        for c in range(HT):
+            cols = slice(N_TILE * c, N_TILE * (c + 1))
+            if c % 2 == 0:
+                nc.vector.tensor_copy(out=osb[:, cols], in_=out_acc[c][:])
+            else:
+                nc.scalar.copy(out=osb[:, cols], in_=out_acc[c][:])
+            nc.sync.dma_start(out=out_flat[:, cols], in_=osb[:, cols])

@@ -26,11 +26,13 @@ HT = H // N_TILE
 FLOPS = 2 * P * (2 * H * F + F * H)
 
 
-def load_scale_rows(nc, plane, scales, groups):
+def load_scale_rows(nc, plane, scales, g0, g1, coarse, fine, fine_rows):
     rows = scales.rearrange("g (h q) w -> q h g w", h=2)
     for q in range(8):
         first = 32 * (q // 4) + q % 4
-        nc.sync.dma_start(out=plane[first:P:64, groups, :], in_=rows[q, :, groups, :])
+        step = coarse if q < 8 - fine_rows else fine
+        for g in range(g0, g1, step):
+            nc.sync.dma_start(out=plane[first:P:64, g : g + step, :], in_=rows[q, :, g : g + step, :])
 
 
 def tile_w4a16tvmmlp_kernel(
@@ -95,8 +97,7 @@ def tile_w4a16tvmmlp_kernel(
 
         nc.sync.dma_start(out=x_sb[:], in_=x.flatten_outer_dims())
         nc.sync.dma_start(out=wg_i[:, 0, :], in_=gw_d[0])
-        load_scale_rows(nc, sg_i, gs_d, slice(0, 2))
-        load_scale_rows(nc, sg_i, gs_d, slice(2, 4))
+        load_scale_rows(nc, sg_i, gs_d, 0, GH, 4, 1, 2)
         for g in range(1, GH):
             nc.sync.dma_start(out=wg_i[:, g, :], in_=gw_d[g])
 
@@ -122,8 +123,7 @@ def tile_w4a16tvmmlp_kernel(
         nc.vector.quantize_mx(out=xq[:].bitcast(FP8X4), scales=xs[:], in_=xg[:])
 
         nc.vector.memset(su[:].bitcast(I32), 0)
-        load_scale_rows(nc, su_i, us_d, slice(0, 2))
-        load_scale_rows(nc, su_i, us_d, slice(2, 4))
+        load_scale_rows(nc, su_i, us_d, 0, GH, 4, 1, 2)
         half = F // 4
         for h in range(2):
             for g in range(GH):
@@ -132,8 +132,7 @@ def tile_w4a16tvmmlp_kernel(
                     in_=uw_d[g][:, half * h : half * (h + 1)],
                 )
         nc.vector.memset(sd[:].bitcast(I32), 0)
-        load_scale_rows(nc, sd_i, ds_d, slice(0, 4))
-        load_scale_rows(nc, sd_i, ds_d, slice(4, 8))
+        load_scale_rows(nc, sd_i, ds_d, 0, GF, 4, 2, 2)
         for g in range(GF - 1):
             nc.sync.dma_start(out=wd_i[:, g, :], in_=dw_d[g])
         piece = N_TILE // 2

@@ -26,12 +26,12 @@ HT = H // N_TILE
 FLOPS = 2 * P * (2 * H * F + F * H)
 
 
-def load_scale_rows(nc, plane, scales, g0, g1, coarse, fine, fine_rows):
+def load_scale_rows(nc, plane, scales, coarse, fine, fine_rows):
     rows = scales.rearrange("g (h q) w -> q h g w", h=2)
     for q in range(8):
         first = 32 * (q // 4) + q % 4
         step = coarse if q < 8 - fine_rows else fine
-        for g in range(g0, g1, step):
+        for g in range(0, plane.shape[1], step):
             nc.sync.dma_start(out=plane[first:P:64, g : g + step, :], in_=rows[q, :, g : g + step, :])
 
 
@@ -79,7 +79,7 @@ def tile_w4a16tvmmlp_kernel(
         wu_i = wu[:].bitcast(I32).rearrange("p (g w) -> p g w", g=GH)
         wd_i = wd[:].bitcast(I32).rearrange("p (g w) -> p g w", g=GF)
         sg_i = sg[:].bitcast(I32).rearrange("p (g w) -> p g w", g=GH)
-        su_i = su[:].bitcast(I32).rearrange("p (g w) -> p g w", g=GH)
+        su_i = su[:].bitcast(I32).rearrange("p (k w) -> p k w", k=2 * GH)
         sd_i = sd[:].bitcast(I32).rearrange("p (g w) -> p g w", g=GF)
         gw_d = gate_W_words.bitcast(I32)
         uw_d = up_W_words.bitcast(I32)
@@ -97,7 +97,7 @@ def tile_w4a16tvmmlp_kernel(
 
         nc.sync.dma_start(out=x_sb[:], in_=x.flatten_outer_dims())
         nc.sync.dma_start(out=wg_i[:, 0, :], in_=gw_d[0])
-        load_scale_rows(nc, sg_i, gs_d, 0, GH, 4, 1, 2)
+        load_scale_rows(nc, sg_i, gs_d, 4, 1, 2)
         for g in range(1, GH):
             nc.sync.dma_start(out=wg_i[:, g, :], in_=gw_d[g])
 
@@ -123,18 +123,25 @@ def tile_w4a16tvmmlp_kernel(
         nc.vector.quantize_mx(out=xq[:].bitcast(FP8X4), scales=xs[:], in_=xg[:])
 
         nc.vector.memset(su[:].bitcast(I32), 0)
-        load_scale_rows(nc, su_i, us_d, 0, GH, 4, 1, 2)
-        half = F // 4
+        half_w = F // 4
+        half_s = F // 8
         for h in range(2):
+            load_scale_rows(nc, su_i[:, GH * h : GH * (h + 1), :], us_d[:, :, half_s * h : half_s * (h + 1)], 4, 2, 4)
             for g in range(GH):
                 nc.sync.dma_start(
-                    out=wu_i[:, g, half * h : half * (h + 1)],
-                    in_=uw_d[g][:, half * h : half * (h + 1)],
+                    out=wu_i[:, g, half_w * h : half_w * (h + 1)],
+                    in_=uw_d[g][:, half_w * h : half_w * (h + 1)],
                 )
+
         nc.vector.memset(sd[:].bitcast(I32), 0)
-        load_scale_rows(nc, sd_i, ds_d, 0, GF, 4, 2, 2)
-        for g in range(GF - 1):
+        load_scale_rows(nc, sd_i[:, 0:4, :], ds_d[0:4], 4, 2, 4)
+        for g in range(0, 4):
             nc.sync.dma_start(out=wd_i[:, g, :], in_=dw_d[g])
+        load_scale_rows(nc, sd_i[:, 4:6, :], ds_d[4:6], 2, 2, 0)
+        for g in range(4, 6):
+            nc.sync.dma_start(out=wd_i[:, g, :], in_=dw_d[g])
+        load_scale_rows(nc, sd_i[:, 6:8, :], ds_d[6:8], 2, 2, 0)
+        nc.sync.dma_start(out=wd_i[:, 6, :], in_=dw_d[6])
         piece = N_TILE // 2
         for c in range(HT):
             nc.sync.dma_start(
@@ -142,13 +149,13 @@ def tile_w4a16tvmmlp_kernel(
                 in_=dw_d[GF - 1][:, piece * c : piece * (c + 1)],
             )
 
-        def stage1_pass(acc, words, plane, g, j):
+        def stage1_pass(acc, words, plane, at, g, j):
             nc.tensor.matmul_mx(
                 out=acc[:],
                 lhsT=xq[:, P * g : P * (g + 1)].bitcast(FP8X4),
                 lhsT_scale=xs[:, P * g : P * (g + 1)],
                 rhs=words[:, 2 * F * g + 2 * N_TILE * j : 2 * F * g + 2 * N_TILE * (j + 1)].bitcast(FP4X4),
-                rhs_scale=plane[:, F * g + N_TILE * j : F * g + N_TILE * (j + 1)],
+                rhs_scale=plane[:, at : at + N_TILE],
                 start=(g == 0),
                 stop=(g == GH - 1),
             )
@@ -156,7 +163,7 @@ def tile_w4a16tvmmlp_kernel(
         gate_acc = [bank(j, F32, "gate%d" % j) for j in range(FT)]
         for g in range(GH):
             for j in range(FT):
-                stage1_pass(gate_acc[j], wg, sg, g, j)
+                stage1_pass(gate_acc[j], wg, sg, F * g + N_TILE * j, g, j)
         for j in range(FT):
             nc.scalar.activation(
                 out=gel[:, N_TILE * j : N_TILE * (j + 1)],
@@ -169,7 +176,7 @@ def tile_w4a16tvmmlp_kernel(
             tiles = range(4 * h, 4 * (h + 1))
             for g in range(GH):
                 for j in tiles:
-                    stage1_pass(up_acc[j], wu, su, g, j)
+                    stage1_pass(up_acc[j], wu, su, (F // 2) * (GH * h + g) + N_TILE * (j % 4), g, j)
             for j in tiles:
                 nc.vector.tensor_tensor(
                     out=inter[:, N_TILE * j : N_TILE * (j + 1)],
@@ -177,24 +184,23 @@ def tile_w4a16tvmmlp_kernel(
                     in1=up_acc[j][:],
                     op=ALU.mult,
                 )
-
-        for j in range(GF):
-            iT = bank(j % 4, BF16, "iT%d" % j)
-            for t in range(4):
-                nc.tensor.transpose(
-                    iT[:, P * t : P * (t + 1)],
-                    inter[:, K_PASS * j + t : K_PASS * (j + 1) : 4],
-                    ident_b[:],
+            for j in tiles:
+                iT = bank(j % 4, BF16, "iT%d" % j)
+                for t in range(4):
+                    nc.tensor.transpose(
+                        iT[:, P * t : P * (t + 1)],
+                        inter[:, K_PASS * j + t : K_PASS * (j + 1) : 4],
+                        ident_b[:],
+                    )
+                nc.scalar.copy(
+                    out=ig[:, K_PASS * j : K_PASS * (j + 1)].rearrange("p (r t) -> p r t", t=4),
+                    in_=iT[:].rearrange("p (t r) -> p r t", t=4),
                 )
-            nc.scalar.copy(
-                out=ig[:, K_PASS * j : K_PASS * (j + 1)].rearrange("p (r t) -> p r t", t=4),
-                in_=iT[:].rearrange("p (t r) -> p r t", t=4),
-            )
-            nc.vector.quantize_mx(
-                out=iq[:, P * j : P * (j + 1)].bitcast(FP8X4),
-                scales=isc[:, P * j : P * (j + 1)],
-                in_=ig[:, K_PASS * j : K_PASS * (j + 1)],
-            )
+                nc.vector.quantize_mx(
+                    out=iq[:, P * j : P * (j + 1)].bitcast(FP8X4),
+                    scales=isc[:, P * j : P * (j + 1)],
+                    in_=ig[:, K_PASS * j : K_PASS * (j + 1)],
+                )
 
         out_acc = [bank(4 + c, F32, "out%d" % c) for c in range(HT)]
         for g in range(GF):

@@ -26,13 +26,11 @@ HT = H // N_TILE
 FLOPS = 2 * P * (2 * H * F + F * H)
 
 
-def load_scale_rows(nc, plane, scales, coarse, fine, fine_rows):
+def load_scale_rows(nc, plane, scales, groups):
     rows = scales.rearrange("g (h q) w -> q h g w", h=2)
     for q in range(8):
         first = 32 * (q // 4) + q % 4
-        step = coarse if q < 8 - fine_rows else fine
-        for g in range(0, plane.shape[1], step):
-            nc.sync.dma_start(out=plane[first:P:64, g : g + step, :], in_=rows[q, :, g : g + step, :])
+        nc.sync.dma_start(out=plane[first:P:64, groups, :], in_=rows[q, :, groups, :])
 
 
 def tile_w4a16tvmmlp_kernel(
@@ -79,7 +77,7 @@ def tile_w4a16tvmmlp_kernel(
         wu_i = wu[:].bitcast(I32).rearrange("p (g w) -> p g w", g=GH)
         wd_i = wd[:].bitcast(I32).rearrange("p (g w) -> p g w", g=GF)
         sg_i = sg[:].bitcast(I32).rearrange("p (g w) -> p g w", g=GH)
-        su_i = su[:].bitcast(I32).rearrange("p (k w) -> p k w", k=2 * GH)
+        su_i = su[:].bitcast(I32).rearrange("p (g w) -> p g w", g=GH)
         sd_i = sd[:].bitcast(I32).rearrange("p (g w) -> p g w", g=GF)
         gw_d = gate_W_words.bitcast(I32)
         uw_d = up_W_words.bitcast(I32)
@@ -97,7 +95,8 @@ def tile_w4a16tvmmlp_kernel(
 
         nc.sync.dma_start(out=x_sb[:], in_=x.flatten_outer_dims())
         nc.sync.dma_start(out=wg_i[:, 0, :], in_=gw_d[0])
-        load_scale_rows(nc, sg_i, gs_d, 4, 1, 2)
+        load_scale_rows(nc, sg_i, gs_d, slice(0, 2))
+        load_scale_rows(nc, sg_i, gs_d, slice(2, 4))
         for g in range(1, GH):
             nc.sync.dma_start(out=wg_i[:, g, :], in_=gw_d[g])
 
@@ -123,25 +122,20 @@ def tile_w4a16tvmmlp_kernel(
         nc.vector.quantize_mx(out=xq[:].bitcast(FP8X4), scales=xs[:], in_=xg[:])
 
         nc.vector.memset(su[:].bitcast(I32), 0)
-        half_w = F // 4
-        half_s = F // 8
+        load_scale_rows(nc, su_i, us_d, slice(0, 2))
+        load_scale_rows(nc, su_i, us_d, slice(2, 4))
+        half = F // 4
         for h in range(2):
-            load_scale_rows(nc, su_i[:, GH * h : GH * (h + 1), :], us_d[:, :, half_s * h : half_s * (h + 1)], 4, 2, 4)
             for g in range(GH):
                 nc.sync.dma_start(
-                    out=wu_i[:, g, half_w * h : half_w * (h + 1)],
-                    in_=uw_d[g][:, half_w * h : half_w * (h + 1)],
+                    out=wu_i[:, g, half * h : half * (h + 1)],
+                    in_=uw_d[g][:, half * h : half * (h + 1)],
                 )
-
         nc.vector.memset(sd[:].bitcast(I32), 0)
-        load_scale_rows(nc, sd_i[:, 0:4, :], ds_d[0:4], 4, 2, 4)
-        for g in range(0, 4):
+        load_scale_rows(nc, sd_i, ds_d, slice(0, 4))
+        load_scale_rows(nc, sd_i, ds_d, slice(4, 8))
+        for g in range(GF - 1):
             nc.sync.dma_start(out=wd_i[:, g, :], in_=dw_d[g])
-        load_scale_rows(nc, sd_i[:, 4:6, :], ds_d[4:6], 2, 2, 0)
-        for g in range(4, 6):
-            nc.sync.dma_start(out=wd_i[:, g, :], in_=dw_d[g])
-        load_scale_rows(nc, sd_i[:, 6:8, :], ds_d[6:8], 2, 2, 0)
-        nc.sync.dma_start(out=wd_i[:, 6, :], in_=dw_d[6])
         piece = N_TILE // 2
         for c in range(HT):
             nc.sync.dma_start(
@@ -149,13 +143,13 @@ def tile_w4a16tvmmlp_kernel(
                 in_=dw_d[GF - 1][:, piece * c : piece * (c + 1)],
             )
 
-        def stage1_pass(acc, words, plane, at, g, j):
+        def stage1_pass(acc, words, plane, g, j):
             nc.tensor.matmul_mx(
                 out=acc[:],
                 lhsT=xq[:, P * g : P * (g + 1)].bitcast(FP8X4),
                 lhsT_scale=xs[:, P * g : P * (g + 1)],
                 rhs=words[:, 2 * F * g + 2 * N_TILE * j : 2 * F * g + 2 * N_TILE * (j + 1)].bitcast(FP4X4),
-                rhs_scale=plane[:, at : at + N_TILE],
+                rhs_scale=plane[:, F * g + N_TILE * j : F * g + N_TILE * (j + 1)],
                 start=(g == 0),
                 stop=(g == GH - 1),
             )
@@ -163,7 +157,7 @@ def tile_w4a16tvmmlp_kernel(
         gate_acc = [bank(j, F32, "gate%d" % j) for j in range(FT)]
         for g in range(GH):
             for j in range(FT):
-                stage1_pass(gate_acc[j], wg, sg, F * g + N_TILE * j, g, j)
+                stage1_pass(gate_acc[j], wg, sg, g, j)
         for j in range(FT):
             nc.scalar.activation(
                 out=gel[:, N_TILE * j : N_TILE * (j + 1)],
@@ -176,7 +170,7 @@ def tile_w4a16tvmmlp_kernel(
             tiles = range(4 * h, 4 * (h + 1))
             for g in range(GH):
                 for j in tiles:
-                    stage1_pass(up_acc[j], wu, su, (F // 2) * (GH * h + g) + N_TILE * (j % 4), g, j)
+                    stage1_pass(up_acc[j], wu, su, g, j)
             for j in tiles:
                 nc.vector.tensor_tensor(
                     out=inter[:, N_TILE * j : N_TILE * (j + 1)],
@@ -184,40 +178,46 @@ def tile_w4a16tvmmlp_kernel(
                     in1=up_acc[j][:],
                     op=ALU.mult,
                 )
-            for j in tiles:
-                iT = bank(j % 4, BF16, "iT%d" % j)
-                for t in range(4):
-                    nc.tensor.transpose(
-                        iT[:, P * t : P * (t + 1)],
-                        inter[:, K_PASS * j + t : K_PASS * (j + 1) : 4],
-                        ident_b[:],
-                    )
-                nc.scalar.copy(
-                    out=ig[:, K_PASS * j : K_PASS * (j + 1)].rearrange("p (r t) -> p r t", t=4),
-                    in_=iT[:].rearrange("p (t r) -> p r t", t=4),
+
+        for j in range(GF):
+            iT = bank(j % 4, BF16, "iT%d" % j)
+            for t in range(4):
+                nc.tensor.transpose(
+                    iT[:, P * t : P * (t + 1)],
+                    inter[:, K_PASS * j + t : K_PASS * (j + 1) : 4],
+                    ident_b[:],
                 )
-                nc.vector.quantize_mx(
-                    out=iq[:, P * j : P * (j + 1)].bitcast(FP8X4),
-                    scales=isc[:, P * j : P * (j + 1)],
-                    in_=ig[:, K_PASS * j : K_PASS * (j + 1)],
-                )
+            nc.scalar.copy(
+                out=ig[:, K_PASS * j : K_PASS * (j + 1)].rearrange("p (r t) -> p r t", t=4),
+                in_=iT[:].rearrange("p (t r) -> p r t", t=4),
+            )
+            nc.vector.quantize_mx(
+                out=iq[:, P * j : P * (j + 1)].bitcast(FP8X4),
+                scales=isc[:, P * j : P * (j + 1)],
+                in_=ig[:, K_PASS * j : K_PASS * (j + 1)],
+            )
 
         out_acc = [bank(4 + c, F32, "out%d" % c) for c in range(HT)]
-        for g in range(GF):
-            for c in range(HT):
-                nc.tensor.matmul_mx(
-                    out=out_acc[c][:],
-                    lhsT=iq[:, P * g : P * (g + 1)].bitcast(FP8X4),
-                    lhsT_scale=isc[:, P * g : P * (g + 1)],
-                    rhs=wd[:, 2 * H * g + 2 * N_TILE * c : 2 * H * g + 2 * N_TILE * (c + 1)].bitcast(FP4X4),
-                    rhs_scale=sd[:, H * g + N_TILE * c : H * g + N_TILE * (c + 1)],
-                    start=(g == 0),
-                    stop=(g == GF - 1),
-                )
+        order = [(g, c) for g in range(GF - 2) for c in range(HT)]
+        order += [(g, c) for c in range(HT) for g in range(GF - 2, GF)]
+        for g, c in order:
+            nc.tensor.matmul_mx(
+                out=out_acc[c][:],
+                lhsT=iq[:, P * g : P * (g + 1)].bitcast(FP8X4),
+                lhsT_scale=isc[:, P * g : P * (g + 1)],
+                rhs=wd[:, 2 * H * g + 2 * N_TILE * c : 2 * H * g + 2 * N_TILE * (c + 1)].bitcast(FP4X4),
+                rhs_scale=sd[:, H * g + N_TILE * c : H * g + N_TILE * (c + 1)],
+                start=(g == 0),
+                stop=(g == GF - 1),
+            )
         for c in range(HT):
-            cols = slice(N_TILE * c, N_TILE * (c + 1))
-            if c % 2 == 0:
-                nc.vector.tensor_copy(out=osb[:, cols], in_=out_acc[c][:])
-            else:
-                nc.scalar.copy(out=osb[:, cols], in_=out_acc[c][:])
-            nc.sync.dma_start(out=out_flat[:, cols], in_=osb[:, cols])
+            parts = 2 if c == HT - 1 else 1
+            width = N_TILE // parts
+            for i in range(parts):
+                cols = slice(N_TILE * c + width * i, N_TILE * c + width * (i + 1))
+                src = out_acc[c][:, width * i : width * (i + 1)]
+                if c % 2 == 0:
+                    nc.vector.tensor_copy(out=osb[:, cols], in_=src)
+                else:
+                    nc.scalar.copy(out=osb[:, cols], in_=src)
+                nc.sync.dma_start(out=out_flat[:, cols], in_=osb[:, cols])

@@ -26,11 +26,14 @@ HT = H // N_TILE
 FLOPS = 2 * P * (2 * H * F + F * H)
 
 
-def load_scale_rows(nc, plane, scales, groups):
+def load_scale_rows(nc, plane, scales):
     rows = scales.rearrange("g (h q) w -> q h g w", h=2)
+    groups = plane.shape[1]
     for q in range(8):
         first = 32 * (q // 4) + q % 4
-        nc.sync.dma_start(out=plane[first:P:64, groups, :], in_=rows[q, :, groups, :])
+        step = groups // (1, 1, 1, 1, 1, 1, 2, 4)[q]
+        for g in range(0, groups, step):
+            nc.sync.dma_start(out=plane[first:P:64, g : g + step, :], in_=rows[q, :, g : g + step, :])
 
 
 def tile_w4a16tvmmlp_kernel(
@@ -95,8 +98,7 @@ def tile_w4a16tvmmlp_kernel(
 
         nc.sync.dma_start(out=x_sb[:], in_=x.flatten_outer_dims())
         nc.sync.dma_start(out=wg_i[:, 0, :], in_=gw_d[0])
-        load_scale_rows(nc, sg_i, gs_d, slice(0, 2))
-        load_scale_rows(nc, sg_i, gs_d, slice(2, 4))
+        load_scale_rows(nc, sg_i, gs_d)
         for g in range(1, GH):
             nc.sync.dma_start(out=wg_i[:, g, :], in_=gw_d[g])
 
@@ -122,8 +124,7 @@ def tile_w4a16tvmmlp_kernel(
         nc.vector.quantize_mx(out=xq[:].bitcast(FP8X4), scales=xs[:], in_=xg[:])
 
         nc.vector.memset(su[:].bitcast(I32), 0)
-        load_scale_rows(nc, su_i, us_d, slice(0, 2))
-        load_scale_rows(nc, su_i, us_d, slice(2, 4))
+        load_scale_rows(nc, su_i, us_d)
         half = F // 4
         for h in range(2):
             for g in range(GH):
@@ -132,8 +133,7 @@ def tile_w4a16tvmmlp_kernel(
                     in_=uw_d[g][:, half * h : half * (h + 1)],
                 )
         nc.vector.memset(sd[:].bitcast(I32), 0)
-        load_scale_rows(nc, sd_i, ds_d, slice(0, 4))
-        load_scale_rows(nc, sd_i, ds_d, slice(4, 8))
+        load_scale_rows(nc, sd_i, ds_d)
         for g in range(GF - 1):
             nc.sync.dma_start(out=wd_i[:, g, :], in_=dw_d[g])
         piece = N_TILE // 2

@@ -26,14 +26,16 @@ HT = H // N_TILE
 FLOPS = 2 * P * (2 * H * F + F * H)
 
 
-def load_scale_rows(nc, plane, scales):
+MARK_AFTER = 4
+
+
+def load_scale_rows(nc, plane, scales, marker):
     rows = scales.rearrange("g (h q) w -> q h g w", h=2)
-    groups = plane.shape[1]
     for q in range(8):
         first = 32 * (q // 4) + q % 4
-        step = groups // (1, 1, 1, 1, 1, 1, 2, 4)[q]
-        for g in range(0, groups, step):
-            nc.sync.dma_start(out=plane[first:P:64, g : g + step, :], in_=rows[q, :, g : g + step, :])
+        nc.sync.dma_start(out=plane[first:P:64, :, :], in_=rows[q])
+        if q + 1 == MARK_AFTER:
+            nc.sync.dma_start(out=marker[0:P:64, :], in_=rows[0, :, 0, 0:16])
 
 
 def tile_w4a16tvmmlp_kernel(
@@ -75,6 +77,9 @@ def tile_w4a16tvmmlp_kernel(
         iq = keep.tile([P, GF * P], U32, name="iq", align_bytes=64)
         isc = keep.tile([P, GF * P], U8, name="isc", align_bytes=64)
         osb = keep.tile([P, H], F32, name="osb")
+        mark_g = keep.tile([P, 16], I32, name="mark_g")
+        mark_u = keep.tile([P, 16], I32, name="mark_u")
+        mark_d = keep.tile([P, 16], I32, name="mark_d")
 
         wg_i = wg[:].bitcast(I32).rearrange("p (g w) -> p g w", g=GH)
         wu_i = wu[:].bitcast(I32).rearrange("p (g w) -> p g w", g=GH)
@@ -98,9 +103,7 @@ def tile_w4a16tvmmlp_kernel(
 
         nc.sync.dma_start(out=x_sb[:], in_=x.flatten_outer_dims())
         nc.sync.dma_start(out=wg_i[:, 0, :], in_=gw_d[0])
-        load_scale_rows(nc, sg_i, gs_d)
-        for g in range(1, GH):
-            nc.sync.dma_start(out=wg_i[:, g, :], in_=gw_d[g])
+        load_scale_rows(nc, sg_i, gs_d, mark_g)
 
         x_words = x_sb[:].bitcast(F32)
         xg_words = xg[:].bitcast(F32)
@@ -124,7 +127,12 @@ def tile_w4a16tvmmlp_kernel(
         nc.vector.quantize_mx(out=xq[:].bitcast(FP8X4), scales=xs[:], in_=xg[:])
 
         nc.vector.memset(su[:].bitcast(I32), 0)
-        load_scale_rows(nc, su_i, us_d)
+        nc.vector.tensor_copy(out=wg_i[0:1, 1, 0:1], in_=mark_g[0:1, 0:1])
+        for g in range(1, GH):
+            nc.sync.dma_start(out=wg_i[:, g, :], in_=gw_d[g])
+        load_scale_rows(nc, su_i, us_d, mark_u)
+        nc.vector.memset(sd[:].bitcast(I32), 0)
+        nc.vector.tensor_copy(out=wu_i[0:1, 0, 0:1], in_=mark_u[0:1, 0:1])
         half = F // 4
         for h in range(2):
             for g in range(GH):
@@ -132,16 +140,7 @@ def tile_w4a16tvmmlp_kernel(
                     out=wu_i[:, g, half * h : half * (h + 1)],
                     in_=uw_d[g][:, half * h : half * (h + 1)],
                 )
-        nc.vector.memset(sd[:].bitcast(I32), 0)
-        load_scale_rows(nc, sd_i, ds_d)
-        for g in range(GF - 1):
-            nc.sync.dma_start(out=wd_i[:, g, :], in_=dw_d[g])
-        piece = N_TILE // 2
-        for c in range(HT):
-            nc.sync.dma_start(
-                out=wd_i[:, GF - 1, piece * c : piece * (c + 1)],
-                in_=dw_d[GF - 1][:, piece * c : piece * (c + 1)],
-            )
+        load_scale_rows(nc, sd_i, ds_d, mark_d)
 
         def stage1_pass(acc, words, plane, g, j):
             nc.tensor.matmul_mx(
@@ -178,6 +177,16 @@ def tile_w4a16tvmmlp_kernel(
                     in1=up_acc[j][:],
                     op=ALU.mult,
                 )
+
+        nc.vector.tensor_copy(out=wd_i[0:1, 0, 0:1], in_=mark_d[0:1, 0:1])
+        for g in range(GF - 1):
+            nc.sync.dma_start(out=wd_i[:, g, :], in_=dw_d[g])
+        piece = N_TILE // 2
+        for c in range(HT):
+            nc.sync.dma_start(
+                out=wd_i[:, GF - 1, piece * c : piece * (c + 1)],
+                in_=dw_d[GF - 1][:, piece * c : piece * (c + 1)],
+            )
 
         for j in range(GF):
             iT = bank(j % 4, BF16, "iT%d" % j)

@@ -26,7 +26,7 @@ HT = H // N_TILE
 FLOPS = 2 * P * (2 * H * F + F * H)
 
 
-MARK_AFTER = 4
+MARK_AFTER = 2
 
 
 def load_scale_rows(nc, plane, scales, marker):

@@ -26,16 +26,14 @@ HT = H // N_TILE
 FLOPS = 2 * P * (2 * H * F + F * H)
 
 
-MARK_AFTER = 2
-
-
-def load_scale_rows(nc, plane, scales, marker):
+def load_scale_rows(nc, plane, scales):
     rows = scales.rearrange("g (h q) w -> q h g w", h=2)
+    groups = plane.shape[1]
     for q in range(8):
         first = 32 * (q // 4) + q % 4
-        nc.sync.dma_start(out=plane[first:P:64, :, :], in_=rows[q])
-        if q + 1 == MARK_AFTER:
-            nc.sync.dma_start(out=marker[0:P:64, :], in_=rows[0, :, 0, 0:16])
+        step = groups // (1, 1, 1, 1, 1, 2, 2, 4)[q]
+        for g in range(0, groups, step):
+            nc.sync.dma_start(out=plane[first:P:64, g : g + step, :], in_=rows[q, :, g : g + step, :])
 
 
 def tile_w4a16tvmmlp_kernel(
@@ -77,9 +75,6 @@ def tile_w4a16tvmmlp_kernel(
         iq = keep.tile([P, GF * P], U32, name="iq", align_bytes=64)
         isc = keep.tile([P, GF * P], U8, name="isc", align_bytes=64)
         osb = keep.tile([P, H], F32, name="osb")
-        mark_g = keep.tile([P, 16], I32, name="mark_g")
-        mark_u = keep.tile([P, 16], I32, name="mark_u")
-        mark_d = keep.tile([P, 16], I32, name="mark_d")
 
         wg_i = wg[:].bitcast(I32).rearrange("p (g w) -> p g w", g=GH)
         wu_i = wu[:].bitcast(I32).rearrange("p (g w) -> p g w", g=GH)
@@ -103,7 +98,9 @@ def tile_w4a16tvmmlp_kernel(
 
         nc.sync.dma_start(out=x_sb[:], in_=x.flatten_outer_dims())
         nc.sync.dma_start(out=wg_i[:, 0, :], in_=gw_d[0])
-        load_scale_rows(nc, sg_i, gs_d, mark_g)
+        load_scale_rows(nc, sg_i, gs_d)
+        for g in range(1, GH):
+            nc.sync.dma_start(out=wg_i[:, g, :], in_=gw_d[g])
 
         x_words = x_sb[:].bitcast(F32)
         xg_words = xg[:].bitcast(F32)
@@ -127,12 +124,7 @@ def tile_w4a16tvmmlp_kernel(
         nc.vector.quantize_mx(out=xq[:].bitcast(FP8X4), scales=xs[:], in_=xg[:])
 
         nc.vector.memset(su[:].bitcast(I32), 0)
-        nc.vector.tensor_copy(out=wg_i[0:1, 1, 0:1], in_=mark_g[0:1, 0:1])
-        for g in range(1, GH):
-            nc.sync.dma_start(out=wg_i[:, g, :], in_=gw_d[g])
-        load_scale_rows(nc, su_i, us_d, mark_u)
-        nc.vector.memset(sd[:].bitcast(I32), 0)
-        nc.vector.tensor_copy(out=wu_i[0:1, 0, 0:1], in_=mark_u[0:1, 0:1])
+        load_scale_rows(nc, su_i, us_d)
         half = F // 4
         for h in range(2):
             for g in range(GH):
@@ -140,7 +132,16 @@ def tile_w4a16tvmmlp_kernel(
                     out=wu_i[:, g, half * h : half * (h + 1)],
                     in_=uw_d[g][:, half * h : half * (h + 1)],
                 )
-        load_scale_rows(nc, sd_i, ds_d, mark_d)
+        nc.vector.memset(sd[:].bitcast(I32), 0)
+        load_scale_rows(nc, sd_i, ds_d)
+        for g in range(GF - 1):
+            nc.sync.dma_start(out=wd_i[:, g, :], in_=dw_d[g])
+        piece = N_TILE // 2
+        for c in range(HT):
+            nc.sync.dma_start(
+                out=wd_i[:, GF - 1, piece * c : piece * (c + 1)],
+                in_=dw_d[GF - 1][:, piece * c : piece * (c + 1)],
+            )
 
         def stage1_pass(acc, words, plane, g, j):
             nc.tensor.matmul_mx(
@@ -177,16 +178,6 @@ def tile_w4a16tvmmlp_kernel(
                     in1=up_acc[j][:],
                     op=ALU.mult,
                 )
-
-        nc.vector.tensor_copy(out=wd_i[0:1, 0, 0:1], in_=mark_d[0:1, 0:1])
-        for g in range(GF - 1):
-            nc.sync.dma_start(out=wd_i[:, g, :], in_=dw_d[g])
-        piece = N_TILE // 2
-        for c in range(HT):
-            nc.sync.dma_start(
-                out=wd_i[:, GF - 1, piece * c : piece * (c + 1)],
-                in_=dw_d[GF - 1][:, piece * c : piece * (c + 1)],
-            )
 
         for j in range(GF):
             iT = bank(j % 4, BF16, "iT%d" % j)

from contextlib import ExitStack

import concourse.mybir as mybir
from concourse.masks import make_identity

F32 = mybir.dt.float32
BF16 = mybir.dt.bfloat16
I32 = mybir.dt.int32
U32 = mybir.dt.uint32
U8 = mybir.dt.uint8
FP8X4 = mybir.dt.float8_e4m3fn_x4
FP4X4 = mybir.dt.float4_e2m1fn_x4
ACT = mybir.ActivationFunctionType
ALU = mybir.AluOpType

P = 128
H = 2048
F = 4096
K_PASS = 512
GH = H // K_PASS
GF = F // K_PASS
N_TILE = 512
FT = F // N_TILE
HT = H // N_TILE

FLOPS = 2 * P * (2 * H * F + F * H)


def load_scale_rows(nc, plane, scales):
    rows = scales.rearrange("g (h q) w -> q h g w", h=2)
    groups = plane.shape[1]
    for q in range(8):
        first = 32 * (q // 4) + q % 4
        step = groups // (1, 1, 1, 1, 1, 2, 2, 4)[q]
        for g in range(0, groups, step):
            nc.sync.dma_start(out=plane[first:P:64, g : g + step, :], in_=rows[q, :, g : g + step, :])


def tile_w4a16tvmmlp_kernel(
    tc,
    x,
    gate_W_words,
    gate_W_scales,
    up_W_words,
    up_W_scales,
    down_W_words,
    down_W_scales,
    out,
):
    nc = tc.nc
    with ExitStack() as ctx:
        keep = ctx.enter_context(tc.tile_pool(name="keep", bufs=1))
        psum = ctx.enter_context(tc.psum_pool(name="psum", bufs=1))
        ctx.enter_context(tc.manual_schedule())

        def bank(i, dtype, name):
            return psum.tile([P, N_TILE], dtype, tag="bank%d" % i, name=name)

        x_sb = keep.tile([P, H], BF16, name="x_sb")
        ident_f = keep.tile([P, P], F32, name="ident_f")
        ident_b = keep.tile([P, P], BF16, name="ident_b")
        warm = keep.tile([P, 8], F32, name="warm")
        wg = keep.tile([P, GH * 2 * F], U8, name="wg", align_bytes=64)
        wu = keep.tile([P, GH * 2 * F], U8, name="wu", align_bytes=64)
        wd = keep.tile([P, GF * 2 * H], U8, name="wd", align_bytes=64)
        sg = keep.tile([P, GH * F], U8, name="sg", align_bytes=64)
        su = keep.tile([P, GH * F], U8, name="su", align_bytes=64)
        sd = keep.tile([P, GF * H], U8, name="sd", align_bytes=64)
        xg = keep.tile([P, GH * P * 4], BF16, name="xg", align_bytes=64)
        xq = keep.tile([P, GH * P], U32, name="xq", align_bytes=64)
        xs = keep.tile([P, GH * P], U8, name="xs", align_bytes=64)
        gel = keep.tile([P, F], F32, name="gel")
        inter = keep.tile([P, F], BF16, name="inter")
        ig = keep.tile([P, GF * P * 4], BF16, name="ig", align_bytes=64)
        iq = keep.tile([P, GF * P], U32, name="iq", align_bytes=64)
        isc = keep.tile([P, GF * P], U8, name="isc", align_bytes=64)
        osb = keep.tile([P, H], F32, name="osb")

        wg_i = wg[:].bitcast(I32).rearrange("p (g w) -> p g w", g=GH)
        wu_i = wu[:].bitcast(I32).rearrange("p (g w) -> p g w", g=GH)
        wd_i = wd[:].bitcast(I32).rearrange("p (g w) -> p g w", g=GF)
        sg_i = sg[:].bitcast(I32).rearrange("p (g w) -> p g w", g=GH)
        su_i = su[:].bitcast(I32).rearrange("p (g w) -> p g w", g=GH)
        sd_i = sd[:].bitcast(I32).rearrange("p (g w) -> p g w", g=GF)
        gw_d = gate_W_words.bitcast(I32)
        uw_d = up_W_words.bitcast(I32)
        dw_d = down_W_words.bitcast(I32)
        gs_d = gate_W_scales.bitcast(I32)
        us_d = up_W_scales.bitcast(I32)
        ds_d = down_W_scales.bitcast(I32)
        out_flat = out.flatten_outer_dims()

        nc.vector.memset(warm[:], 0.0)
        nc.scalar.activation(out=warm[:], in_=warm[:], func=ACT.Gelu_apprx_tanh)
        nc.vector.memset(sg[:].bitcast(I32), 0)
        make_identity(nc, ident_f[:])
        make_identity(nc, ident_b[:])

        nc.sync.dma_start(out=x_sb[:], in_=x.flatten_outer_dims())
        nc.sync.dma_start(out=wg_i[:, 0, :], in_=gw_d[0])
        load_scale_rows(nc, sg_i, gs_d)
        for g in range(1, GH):
            nc.sync.dma_start(out=wg_i[:, g, :], in_=gw_d[g])

        x_words = x_sb[:].bitcast(F32)
        xg_words = xg[:].bitcast(F32)
        for i in range(2):
            xT = bank(i, F32, "xT%d" % i)
            for gg in range(2):
                g = 2 * i + gg
                for u in range(2):
                    col = P * (2 * gg + u)
                    nc.tensor.transpose(
                        xT[:, col : col + P],
                        x_words[:, 256 * g + u : 256 * (g + 1) : 2],
                        ident_f[:],
                    )
            dst = xg_words[:, 512 * i : 512 * (i + 1)].rearrange("p (g r u) -> p g r u", g=2, u=2)
            src = xT[:].rearrange("p (g u r) -> p g r u", g=2, u=2)
            if i == 0:
                nc.vector.tensor_copy(out=dst, in_=src)
            else:
                nc.scalar.copy(out=dst, in_=src)
        nc.vector.quantize_mx(out=xq[:].bitcast(FP8X4), scales=xs[:], in_=xg[:])

        nc.vector.memset(su[:].bitcast(I32), 0)
        load_scale_rows(nc, su_i, us_d)
        half = F // 4
        for h in range(2):
            for g in range(GH):
                nc.sync.dma_start(
                    out=wu_i[:, g, half * h : half * (h + 1)],
                    in_=uw_d[g][:, half * h : half * (h + 1)],
                )
        nc.vector.memset(sd[:].bitcast(I32), 0)
        load_scale_rows(nc, sd_i, ds_d)
        for g in range(GF - 1):
            nc.sync.dma_start(out=wd_i[:, g, :], in_=dw_d[g])
        piece = N_TILE // 2
        for c in range(HT):
            nc.sync.dma_start(
                out=wd_i[:, GF - 1, piece * c : piece * (c + 1)],
                in_=dw_d[GF - 1][:, piece * c : piece * (c + 1)],
            )

        def stage1_pass(acc, words, plane, g, j):
            nc.tensor.matmul_mx(
                out=acc[:],
                lhsT=xq[:, P * g : P * (g + 1)].bitcast(FP8X4),
                lhsT_scale=xs[:, P * g : P * (g + 1)],
                rhs=words[:, 2 * F * g + 2 * N_TILE * j : 2 * F * g + 2 * N_TILE * (j + 1)].bitcast(FP4X4),
                rhs_scale=plane[:, F * g + N_TILE * j : F * g + N_TILE * (j + 1)],
                start=(g == 0),
                stop=(g == GH - 1),
            )

        gate_acc = [bank(j, F32, "gate%d" % j) for j in range(FT)]
        for g in range(GH):
            for j in range(FT):
                stage1_pass(gate_acc[j], wg, sg, g, j)
        for j in range(FT):
            nc.scalar.activation(
                out=gel[:, N_TILE * j : N_TILE * (j + 1)],
                in_=gate_acc[j][:],
                func=ACT.Gelu_apprx_tanh,
            )

        up_acc = [bank(j, F32, "up%d" % j) for j in range(FT)]
        for h in range(2):
            tiles = range(4 * h, 4 * (h + 1))
            for g in range(GH):
                for j in tiles:
                    stage1_pass(up_acc[j], wu, su, g, j)
            for j in tiles:
                nc.vector.tensor_tensor(
                    out=inter[:, N_TILE * j : N_TILE * (j + 1)],
                    in0=gel[:, N_TILE * j : N_TILE * (j + 1)],
                    in1=up_acc[j][:],
                    op=ALU.mult,
                )

        for j in range(GF):
            iT = bank(j % 4, BF16, "iT%d" % j)
            for t in range(4):
                nc.tensor.transpose(
                    iT[:, P * t : P * (t + 1)],
                    inter[:, K_PASS * j + t : K_PASS * (j + 1) : 4],
                    ident_b[:],
                )
            nc.scalar.copy(
                out=ig[:, K_PASS * j : K_PASS * (j + 1)].rearrange("p (r t) -> p r t", t=4),
                in_=iT[:].rearrange("p (t r) -> p r t", t=4),
            )
            nc.vector.quantize_mx(
                out=iq[:, P * j : P * (j + 1)].bitcast(FP8X4),
                scales=isc[:, P * j : P * (j + 1)],
                in_=ig[:, K_PASS * j : K_PASS * (j + 1)],
            )

        out_acc = [bank(4 + c, F32, "out%d" % c) for c in range(HT)]
        order = [(g, c) for g in range(GF - 2) for c in range(HT)]
        order += [(g, c) for c in range(HT) for g in range(GF - 2, GF)]
        for g, c in order:
            nc.tensor.matmul_mx(
                out=out_acc[c][:],
                lhsT=iq[:, P * g : P * (g + 1)].bitcast(FP8X4),
                lhsT_scale=isc[:, P * g : P * (g + 1)],
                rhs=wd[:, 2 * H * g + 2 * N_TILE * c : 2 * H * g + 2 * N_TILE * (c + 1)].bitcast(FP4X4),
                rhs_scale=sd[:, H * g + N_TILE * c : H * g + N_TILE * (c + 1)],
                start=(g == 0),
                stop=(g == GF - 1),
            )
        for c in range(HT):
            parts = 2 if c == HT - 1 else 1
            width = N_TILE // parts
            for i in range(parts):
                cols = slice(N_TILE * c + width * i, N_TILE * c + width * (i + 1))
                src = out_acc[c][:, width * i : width * (i + 1)]
                if c % 2 == 0:
                    nc.vector.tensor_copy(out=osb[:, cols], in_=src)
                else:
                    nc.scalar.copy(out=osb[:, cols], in_=src)
                nc.sync.dma_start(out=out_flat[:, cols], in_=osb[:, cols])
